import numpy as np
import ml_dtypes


def mxq(x, axis, fmt="e4m3"):
    dtype, down = {"e4m3": (ml_dtypes.float8_e4m3fn, 7), "e5m2": (ml_dtypes.float8_e5m2, 14)}[fmt]
    v = np.moveaxis(np.asarray(x, np.float32).astype(ml_dtypes.bfloat16).astype(np.float64), axis, -1)
    blocks = v.reshape(v.shape[:-1] + (-1, 32))
    amax = np.abs(blocks).max(-1, keepdims=True)
    byte = np.maximum(np.where(amax > 0, np.frexp(amax)[1] - 1 + 127, 0) - down, 1)
    scale = np.exp2(byte - 127.0)
    codes = (blocks / scale).astype(np.float32).astype(dtype).astype(np.float64)
    return np.moveaxis((codes * scale).reshape(v.shape), -1, axis)


WIDE = False


def mx_kscale(k):
    if not WIDE:
        return np.ones(k)
    levels = np.array([10, -10, 5, -5, 0])
    a = np.random.permutation(np.resize(levels, k // 512 * 4)).reshape(k // 512, 4)
    idx = np.arange(k)
    return np.exp2(a[idx // 512, idx % 128 // 32])


BF16 = ml_dtypes.bfloat16


def bf(x):
    return np.asarray(x, np.float32).astype(BF16)


def f64(x):
    return np.asarray(x).astype(np.float64)


B, S, D, H, DH, F = 4, 2048, 1024, 2, 64, 4096
E = H * DH
EPS = 1e-5


def layernorm(x, g, b):
    mu = x.mean(-1, keepdims=True)
    var = np.square(x - mu).mean(-1, keepdims=True)
    return (x - mu) / np.sqrt(var + EPS) * g + b


def make_pe():
    position = np.arange(S)[:, None] * 1.0
    div_term = np.exp(np.arange(0, DH, 2) * -(np.log(10000.0) / DH))
    pe = np.zeros((S, DH))
    pe[:, 0::2] = np.sin(position * div_term)
    pe[:, 1::2] = np.cos(position * div_term)
    return pe


def rope(t, pe):
    tr = t.reshape(B, H, S, DH // 2, 2)
    c = pe[:S, 0::2][None, None]
    d = pe[:S, 1::2][None, None]
    t0 = tr[..., 0] * c - tr[..., 1] * d
    t1 = tr[..., 0] * d + tr[..., 1] * c
    return np.stack([t0, t1], axis=-1).reshape(B, H, S, DH)


def setup_inputs():
    s = mx_kscale(D)
    x = np.random.standard_normal((B, S, D)) + 0.5 * np.random.standard_normal((B, S, 1))
    return {"x": bf(x),
            "pe": bf(make_pe()),
            "w_qkv": bf(np.random.standard_normal((3 * E, D)) / np.sqrt(D) / s),
            "g1": bf((1.0 + 0.1 * np.random.standard_normal(D)) * s),
            "b1": bf(0.1 * np.random.standard_normal(D) * s)}


def reference(x, pe, w_qkv, g1, b1):
    h = layernorm(f64(x), f64(g1), f64(b1))
    qkv = mxq(h, 2, "e4m3") @ mxq(f64(w_qkv), 1, "e4m3").T
    qkv = qkv.reshape(B, S, 3, H, DH)
    q, k, v = [qkv[:, :, i].transpose(0, 2, 1, 3) for i in range(3)]
    p = f64(pe)
    return rope(q, p), rope(k, p), v

@@ -1,0 +1,237 @@
+from contextlib import ExitStack
+
+import concourse.mybir as mybir
+from concourse.masks import make_identity
+
+F32 = mybir.dt.float32
+BF16 = mybir.dt.bfloat16
+U32 = mybir.dt.uint32
+U8 = mybir.dt.uint8
+FP8X4 = mybir.dt.float8_e4m3fn_x4
+ALU = mybir.AluOpType
+ACT = mybir.ActivationFunctionType
+
+B, S, D, H, DH = 4, 2048, 1024, 2, 64
+EPS = 1e-5
+P = 128
+PACK = 4
+PASSES = D // (P * PACK)
+CHUNKS = D // P
+SLOTS_PER_BATCH = S // P
+SLOTS = 4
+TOKENS = SLOTS * P
+GROUPS_PER_BATCH = SLOTS_PER_BATCH // SLOTS
+PAIRS = DH // 2
+ROTATED = 2 * H
+QK_COLS = ROTATED * DH
+V_COLS = H * DH
+OUT_COLS = QK_COLS + V_COLS
+BN_MAX = 512
+
+FLOPS = 2 * B * S * D * OUT_COLS
+
+
+def tile_minitransformerlayer_pa_t_kernel(tc, x, pe, w_qkv, g1, b1, out_0, out_1, out_2):
+    nc = tc.nc
+    outs = (out_0, out_1, out_2)
+
+    with ExitStack() as ctx:
+        const = ctx.enter_context(tc.tile_pool(name="const", bufs=1))
+        x_pool = ctx.enter_context(tc.tile_pool(name="x_pool", bufs=3))
+        small = ctx.enter_context(tc.tile_pool(name="small", bufs=3))
+        xn_pool = ctx.enter_context(tc.tile_pool(name="xn_pool", bufs=2))
+        h_pool = ctx.enter_context(tc.tile_pool(name="h_pool", bufs=2))
+        mx_pool = ctx.enter_context(tc.tile_pool(name="mx_pool", bufs=2))
+        rot_pool = ctx.enter_context(tc.tile_pool(name="rot_pool", bufs=2))
+        res_pool = ctx.enter_context(tc.tile_pool(name="res_pool", bufs=3))
+
+        def load_group(group):
+            batch, first_slot = group // GROUPS_PER_BATCH, (group % GROUPS_PER_BATCH) * SLOTS
+            x_sb = x_pool.tile([P, SLOTS, D], BF16, name="x_sb")
+            by_slot = x[batch].rearrange("(p t) k -> p t k", t=SLOTS_PER_BATCH)
+            nc.sync.dma_start(out=x_sb[:], in_=by_slot[:, first_slot : first_slot + SLOTS, :])
+            return x_sb
+
+        x_first = load_group(0)
+
+        ident_f32 = const.tile([P, P], F32, name="ident_f32")
+        make_identity(nc, ident_f32[:])
+        ident_bf16 = const.tile([P, P], BF16, name="ident_bf16")
+        make_identity(nc, ident_bf16[:])
+        eps = const.tile([P, 1], F32, name="eps")
+        nc.vector.memset(eps[:], EPS)
+
+        gb_rows = const.tile([P, P], BF16, name="gb_rows")
+        nc.vector.memset(gb_rows[:], 0.0)
+        nc.sync.dma_start(out=gb_rows[0:CHUNKS, :], in_=g1.rearrange("(c p) -> c p", p=P))
+        nc.sync.dma_start(out=gb_rows[CHUNKS : 2 * CHUNKS, :], in_=b1.rearrange("(c p) -> c p", p=P))
+        w_sb = const.tile([P, OUT_COLS // P, D], BF16, name="w_sb")
+        nc.sync.dma_start(out=w_sb[:], in_=w_qkv.rearrange("(i p) k -> p i k", p=P))
+        pe_sb = const.tile([P, SLOTS_PER_BATCH, PAIRS, 2], BF16, name="pe_sb")
+        nc.sync.dma_start(out=pe_sb[:], in_=pe.rearrange("(p t) (j e) -> p t j e", t=SLOTS_PER_BATCH, e=2))
+
+        c_twice = const.tile([P, SLOTS_PER_BATCH, PAIRS, 2], F32, name="c_twice")
+        nc.vector.tensor_copy(
+            out=c_twice[:], in_=pe_sb[:, :, :, 0:1].to_broadcast([P, SLOTS_PER_BATCH, PAIRS, 2])
+        )
+        d_pos = const.tile([P, SLOTS_PER_BATCH, PAIRS], F32, name="d_pos")
+        nc.vector.tensor_copy(out=d_pos[:], in_=pe_sb[:, :, :, 1])
+        d_neg = const.tile([P, SLOTS_PER_BATCH, PAIRS], F32, name="d_neg")
+        nc.vector.tensor_scalar_mul(out=d_neg[:], in0=pe_sb[:, :, :, 1], scalar1=-1.0)
+
+        gain_bias = const.tile([P, 2 * CHUNKS], F32, name="gain_bias")
+        w_grouped = const.tile([P, PASSES, OUT_COLS, PACK], BF16, name="w_grouped", align_bytes=64)
+        w_codes = const.tile([P, PASSES, OUT_COLS], U32, name="w_codes", align_bytes=64)
+        w_scales = const.tile([P, PASSES, OUT_COLS], U8, name="w_scales", align_bytes=64)
+        with tc.psum_pool(name="setup_psum", bufs=2) as setup_psum:
+            gb_cols = setup_psum.tile([P, P], BF16, name="gb_cols")
+            nc.tensor.transpose(gb_cols[:], gb_rows[:], ident_bf16[:])
+            nc.vector.tensor_copy(out=gain_bias[:], in_=gb_cols[:, 0 : 2 * CHUNKS])
+
+            for u in range(PASSES):
+                for i in range(OUT_COLS // P):
+                    rows = slice(i * P, (i + 1) * P)
+                    w_t = setup_psum.tile([P, PACK, P], BF16, name="w_t")
+                    for t in range(PACK):
+                        chunk = u * PACK + t
+                        nc.tensor.transpose(
+                            w_t[:, t, :], w_sb[:, i, chunk * P : (chunk + 1) * P], ident_bf16[:]
+                        )
+                    nc.vector.tensor_copy(
+                        out=w_grouped[:, u, rows, :], in_=w_t[:].rearrange("p t n -> p n t")
+                    )
+            for u in range(PASSES):
+                for i in range(OUT_COLS // P):
+                    rows = slice(i * P, (i + 1) * P)
+                    nc.vector.quantize_mx(
+                        out=w_codes[:, u, rows].bitcast(FP8X4),
+                        scales=w_scales[:, u, rows],
+                        in_=w_grouped[:, u, rows, :].rearrange("p n t -> p (n t)"),
+                    )
+
+        xt_psum = ctx.enter_context(tc.psum_pool(name="xt_psum", bufs=4))
+        qk_psum = ctx.enter_context(tc.psum_pool(name="qk_psum", bufs=2))
+        v_psum = ctx.enter_context(tc.psum_pool(name="v_psum", bufs=2))
+
+        x_next = x_first
+        for group in range(B * GROUPS_PER_BATCH):
+            batch, first_slot = group // GROUPS_PER_BATCH, (group % GROUPS_PER_BATCH) * SLOTS
+            x_sb = x_next
+            if group + 1 < B * GROUPS_PER_BATCH:
+                x_next = load_group(group + 1)
+
+            stats = small.tile([P, SLOTS, D // BN_MAX, 6], F32, name="stats")
+            mean_var = small.tile([P, SLOTS, 2], F32, name="mean_var")
+            for s in range(SLOTS):
+                for part in range(D // BN_MAX):
+                    nc.vector.bn_stats(
+                        out=stats[:, s, part, :], in_=x_sb[:, s, part * BN_MAX : (part + 1) * BN_MAX]
+                    )
+                nc.vector.bn_aggr(out=mean_var[:, s, :], in_=stats[:, s].rearrange("p a c -> p (a c)"))
+            std = small.tile([P, SLOTS], F32, name="std")
+            nc.scalar.activation(out=std[:], in_=mean_var[:, :, 1], func=ACT.Sqrt, bias=eps[:], scale=1.0)
+            rstd = small.tile([P, SLOTS], F32, name="rstd")
+            nc.vector.reciprocal(out=rstd[:], in_=std[:])
+            neg_mean = small.tile([P, SLOTS], F32, name="neg_mean")
+            nc.vector.tensor_scalar_mul(out=neg_mean[:], in0=mean_var[:, :, 0], scalar1=-1.0)
+
+            xn = xn_pool.tile([P, SLOTS, D], F32, name="xn")
+            for s in range(SLOTS):
+                nc.gpsimd.tensor_scalar(
+                    out=xn[:, s, :],
+                    in0=x_sb[:, s, :],
+                    scalar1=neg_mean[:, s : s + 1],
+                    scalar2=rstd[:, s : s + 1],
+                    op0=ALU.add,
+                    op1=ALU.mult,
+                )
+
+            h_chunks = h_pool.tile([P, CHUNKS, TOKENS], BF16, name="h_chunks")
+            for c in range(CHUNKS):
+                xn_t = xt_psum.tile([P, TOKENS], F32, name="xn_t")
+                for s in range(SLOTS):
+                    nc.tensor.transpose(
+                        xn_t[:, s * P : (s + 1) * P], xn[:, s, c * P : (c + 1) * P], ident_f32[:]
+                    )
+                nc.scalar.activation(
+                    out=h_chunks[:, c, :],
+                    in_=xn_t[:],
+                    func=ACT.Identity,
+                    scale=gain_bias[:, c : c + 1],
+                    bias=gain_bias[:, CHUNKS + c : CHUNKS + c + 1],
+                )
+
+            h_grouped = h_pool.tile([P, PASSES, TOKENS, PACK], BF16, name="h_grouped", align_bytes=64)
+            h_codes = mx_pool.tile([P, PASSES, TOKENS], U32, name="h_codes", align_bytes=64)
+            h_scales = mx_pool.tile([P, PASSES, TOKENS], U8, name="h_scales", align_bytes=64)
+            for u in range(PASSES):
+                nc.scalar.copy(
+                    out=h_grouped[:, u].rearrange("p (n i) t -> p n t i", i=4),
+                    in_=h_chunks[:, u * PACK : (u + 1) * PACK, :].rearrange("p t (n i) -> p n t i", i=4),
+                )
+            for u in range(PASSES):
+                nc.vector.quantize_mx(
+                    out=h_codes[:, u, :].bitcast(FP8X4),
+                    scales=h_scales[:, u, :],
+                    in_=h_grouped[:, u].rearrange("p n t -> p (n t)"),
+                )
+
+            result = res_pool.tile([P, 3 * H, SLOTS, DH], F32, name="result")
+            v_ps = v_psum.tile([P, SLOTS, V_COLS], F32, name="v_ps")
+            for half in range(SLOTS // 2):
+                qk_ps = qk_psum.tile([P, 2, QK_COLS], F32, name="qk_ps")
+                for i in range(2):
+                    s = 2 * half + i
+                    tokens = slice(s * P, (s + 1) * P)
+                    for acc, cols in ((qk_ps[:, i, :], slice(0, QK_COLS)), (v_ps[:, s, :], slice(QK_COLS, OUT_COLS))):
+                        for u in range(PASSES):
+                            nc.tensor.matmul_mx(
+                                out=acc,
+                                lhsT=h_codes[:, u, tokens].bitcast(FP8X4),
+                                lhsT_scale=h_scales[:, u, tokens],
+                                rhs=w_codes[:, u, cols].bitcast(FP8X4),
+                                rhs_scale=w_scales[:, u, cols],
+                                start=(u == 0),
+                                stop=(u == PASSES - 1),
+                            )
+
+                slots = slice(first_slot + 2 * half, first_slot + 2 * half + 2)
+                rotated = result[:, 0:ROTATED, 2 * half : 2 * half + 2, :]
+                nc.vector.tensor_tensor(
+                    out=rotated.rearrange("p a i d -> p i a d"),
+                    in0=qk_ps[:].rearrange("p i (a d) -> p i a d", a=ROTATED),
+                    in1=c_twice[:, slots].rearrange("p i j e -> p i (j e)").unsqueeze(2).to_broadcast([P, 2, ROTATED, DH]),
+                    op=ALU.mult,
+                )
+                by_pair = qk_ps[:].rearrange("p i (a j e) -> p i a j e", a=ROTATED, e=2)
+                crossed = rot_pool.tile([P, 2, 2, ROTATED, PAIRS], F32, name="crossed")
+                nc.vector.tensor_tensor(
+                    out=crossed[:, 0],
+                    in0=by_pair[:, :, :, :, 1],
+                    in1=d_neg[:, slots].unsqueeze(2).to_broadcast([P, 2, ROTATED, PAIRS]),
+                    op=ALU.mult,
+                )
+                nc.vector.tensor_tensor(
+                    out=crossed[:, 1],
+                    in0=by_pair[:, :, :, :, 0],
+                    in1=d_pos[:, slots].unsqueeze(2).to_broadcast([P, 2, ROTATED, PAIRS]),
+                    op=ALU.mult,
+                )
+                nc.gpsimd.tensor_tensor(
+                    out=rotated.rearrange("p a i (j e) -> p i a j e", e=2),
+                    in0=rotated.rearrange("p a i (j e) -> p i a j e", e=2),
+                    in1=crossed[:].rearrange("p e i a j -> p i a j e"),
+                    op=ALU.add,
+                )
+
+            nc.vector.tensor_copy(
+                out=result[:, ROTATED : 3 * H].rearrange("p a s d -> p s a d"),
+                in_=v_ps[:].rearrange("p s (a d) -> p s a d", a=H),
+            )
+
+            for which in range(3):
+                by_slot = outs[which][batch].rearrange("h (p t) d -> p h t d", t=SLOTS_PER_BATCH)
+                nc.sync.dma_start(
+                    out=by_slot[:, :, first_slot : first_slot + SLOTS, :],
+                    in_=result[:, which * H : (which + 1) * H],
+                )

@@ -27,6 +27,8 @@ QK_COLS = ROTATED * DH
 V_COLS = H * DH
 OUT_COLS = QK_COLS + V_COLS
 BN_MAX = 512
+GROUPS = B * GROUPS_PER_BATCH
+LOADS_AHEAD = 2
 
 FLOPS = 2 * B * S * D * OUT_COLS
 
@@ -37,22 +39,25 @@ def tile_minitransformerlayer_pa_t_kernel(tc, x, pe, w_qkv, g1, b1, out_0, out_1
 
     with ExitStack() as ctx:
         const = ctx.enter_context(tc.tile_pool(name="const", bufs=1))
-        x_pool = ctx.enter_context(tc.tile_pool(name="x_pool", bufs=3))
+        x_pool = ctx.enter_context(tc.tile_pool(name="x_pool", bufs=4))
         small = ctx.enter_context(tc.tile_pool(name="small", bufs=3))
         xn_pool = ctx.enter_context(tc.tile_pool(name="xn_pool", bufs=2))
         h_pool = ctx.enter_context(tc.tile_pool(name="h_pool", bufs=2))
         mx_pool = ctx.enter_context(tc.tile_pool(name="mx_pool", bufs=2))
-        rot_pool = ctx.enter_context(tc.tile_pool(name="rot_pool", bufs=2))
+        rot_pool = ctx.enter_context(tc.tile_pool(name="rot_pool", bufs=4))
         res_pool = ctx.enter_context(tc.tile_pool(name="res_pool", bufs=3))
+
+        live = {}
 
         def load_group(group):
             batch, first_slot = group // GROUPS_PER_BATCH, (group % GROUPS_PER_BATCH) * SLOTS
             x_sb = x_pool.tile([P, SLOTS, D], BF16, name="x_sb")
             by_slot = x[batch].rearrange("(p t) k -> p t k", t=SLOTS_PER_BATCH)
             nc.sync.dma_start(out=x_sb[:], in_=by_slot[:, first_slot : first_slot + SLOTS, :])
-            return x_sb
+            live["x", group] = x_sb
 
-        x_first = load_group(0)
+        for group in range(LOADS_AHEAD):
+            load_group(group)
 
         ident_f32 = const.tile([P, P], F32, name="ident_f32")
         make_identity(nc, ident_f32[:])
@@ -113,13 +118,8 @@ def tile_minitransformerlayer_pa_t_kernel(tc, x, pe, w_qkv, g1, b1, out_0, out_1
         qk_psum = ctx.enter_context(tc.psum_pool(name="qk_psum", bufs=2))
         v_psum = ctx.enter_context(tc.psum_pool(name="v_psum", bufs=2))
 
-        x_next = x_first
-        for group in range(B * GROUPS_PER_BATCH):
-            batch, first_slot = group // GROUPS_PER_BATCH, (group % GROUPS_PER_BATCH) * SLOTS
-            x_sb = x_next
-            if group + 1 < B * GROUPS_PER_BATCH:
-                x_next = load_group(group + 1)
-
+        def statistics(group):
+            x_sb = live["x", group]
             stats = small.tile([P, SLOTS, D // BN_MAX, 6], F32, name="stats")
             mean_var = small.tile([P, SLOTS, 2], F32, name="mean_var")
             for s in range(SLOTS):
@@ -128,26 +128,44 @@ def tile_minitransformerlayer_pa_t_kernel(tc, x, pe, w_qkv, g1, b1, out_0, out_1
                         out=stats[:, s, part, :], in_=x_sb[:, s, part * BN_MAX : (part + 1) * BN_MAX]
                     )
                 nc.vector.bn_aggr(out=mean_var[:, s, :], in_=stats[:, s].rearrange("p a c -> p (a c)"))
-            std = small.tile([P, SLOTS], F32, name="std")
-            nc.scalar.activation(out=std[:], in_=mean_var[:, :, 1], func=ACT.Sqrt, bias=eps[:], scale=1.0)
-            rstd = small.tile([P, SLOTS], F32, name="rstd")
-            nc.vector.reciprocal(out=rstd[:], in_=std[:])
-            neg_mean = small.tile([P, SLOTS], F32, name="neg_mean")
-            nc.vector.tensor_scalar_mul(out=neg_mean[:], in0=mean_var[:, :, 0], scalar1=-1.0)
+            live["mean_var", group] = mean_var
 
+        def standard_deviation(group):
+            std = small.tile([P, SLOTS], F32, name="std")
+            nc.scalar.activation(
+                out=std[:], in_=live["mean_var", group][:, :, 1], func=ACT.Sqrt, bias=eps[:], scale=1.0
+            )
+            live["std", group] = std
+
+        def token_scalars(group):
+            rstd = small.tile([P, SLOTS], F32, name="rstd")
+            nc.vector.reciprocal(out=rstd[:], in_=live["std", group][:])
+            neg_mean = small.tile([P, SLOTS], F32, name="neg_mean")
+            nc.vector.tensor_scalar_mul(out=neg_mean[:], in0=live["mean_var", group][:, :, 0], scalar1=-1.0)
+            live["rstd", group] = rstd
+            live["neg_mean", group] = neg_mean
+
+        def normalise(group):
             xn = xn_pool.tile([P, SLOTS, D], F32, name="xn")
             for s in range(SLOTS):
                 nc.gpsimd.tensor_scalar(
                     out=xn[:, s, :],
-                    in0=x_sb[:, s, :],
-                    scalar1=neg_mean[:, s : s + 1],
-                    scalar2=rstd[:, s : s + 1],
+                    in0=live["x", group][:, s, :],
+                    scalar1=live["neg_mean", group][:, s : s + 1],
+                    scalar2=live["rstd", group][:, s : s + 1],
                     op0=ALU.add,
                     op1=ALU.mult,
                 )
+            live["xn", group] = xn
 
-            h_chunks = h_pool.tile([P, CHUNKS, TOKENS], BF16, name="h_chunks")
-            for c in range(CHUNKS):
+        def transpose_and_scale(group, u):
+            if u == 0:
+                live["h_chunks", group] = h_pool.tile([P, CHUNKS, TOKENS], BF16, name="h_chunks")
+                live["h_grouped", group] = h_pool.tile(
+                    [P, PASSES, TOKENS, PACK], BF16, name="h_grouped", align_bytes=64
+                )
+            xn, h_chunks = live["xn", group], live["h_chunks", group]
+            for c in range(u * PACK, (u + 1) * PACK):
                 xn_t = xt_psum.tile([P, TOKENS], F32, name="xn_t")
                 for s in range(SLOTS):
                     nc.tensor.transpose(
@@ -161,29 +179,40 @@ def tile_minitransformerlayer_pa_t_kernel(tc, x, pe, w_qkv, g1, b1, out_0, out_1
                     bias=gain_bias[:, CHUNKS + c : CHUNKS + c + 1],
                 )
 
-            h_grouped = h_pool.tile([P, PASSES, TOKENS, PACK], BF16, name="h_grouped", align_bytes=64)
+        def regroup(group, u):
+            nc.scalar.copy(
+                out=live["h_grouped", group][:, u].rearrange("p (n i) t -> p n t i", i=4),
+                in_=live["h_chunks", group][:, u * PACK : (u + 1) * PACK, :].rearrange(
+                    "p t (n i) -> p n t i", i=4
+                ),
+            )
+
+        def quantise(group):
             h_codes = mx_pool.tile([P, PASSES, TOKENS], U32, name="h_codes", align_bytes=64)
             h_scales = mx_pool.tile([P, PASSES, TOKENS], U8, name="h_scales", align_bytes=64)
-            for u in range(PASSES):
-                nc.scalar.copy(
-                    out=h_grouped[:, u].rearrange("p (n i) t -> p n t i", i=4),
-                    in_=h_chunks[:, u * PACK : (u + 1) * PACK, :].rearrange("p t (n i) -> p n t i", i=4),
-                )
             for u in range(PASSES):
                 nc.vector.quantize_mx(
                     out=h_codes[:, u, :].bitcast(FP8X4),
                     scales=h_scales[:, u, :],
-                    in_=h_grouped[:, u].rearrange("p n t -> p (n t)"),
+                    in_=live["h_grouped", group][:, u].rearrange("p n t -> p (n t)"),
                 )
+            live["h_codes", group] = h_codes
+            live["h_scales", group] = h_scales
 
-            result = res_pool.tile([P, 3 * H, SLOTS, DH], F32, name="result")
+        def project(group):
+            h_codes, h_scales = live["h_codes", group], live["h_scales", group]
             v_ps = v_psum.tile([P, SLOTS, V_COLS], F32, name="v_ps")
+            live["v_ps", group] = v_ps
             for half in range(SLOTS // 2):
                 qk_ps = qk_psum.tile([P, 2, QK_COLS], F32, name="qk_ps")
+                live["qk_ps", group, half] = qk_ps
                 for i in range(2):
                     s = 2 * half + i
                     tokens = slice(s * P, (s + 1) * P)
-                    for acc, cols in ((qk_ps[:, i, :], slice(0, QK_COLS)), (v_ps[:, s, :], slice(QK_COLS, OUT_COLS))):
+                    for acc, cols in (
+                        (qk_ps[:, i, :], slice(0, QK_COLS)),
+                        (v_ps[:, s, :], slice(QK_COLS, OUT_COLS)),
+                    ):
                         for u in range(PASSES):
                             nc.tensor.matmul_mx(
                                 out=acc,
@@ -195,43 +224,93 @@ def tile_minitransformerlayer_pa_t_kernel(tc, x, pe, w_qkv, g1, b1, out_0, out_1
                                 stop=(u == PASSES - 1),
                             )
 
-                slots = slice(first_slot + 2 * half, first_slot + 2 * half + 2)
-                rotated = result[:, 0:ROTATED, 2 * half : 2 * half + 2, :]
-                nc.vector.tensor_tensor(
-                    out=rotated.rearrange("p a i d -> p i a d"),
-                    in0=qk_ps[:].rearrange("p i (a d) -> p i a d", a=ROTATED),
-                    in1=c_twice[:, slots].rearrange("p i j e -> p i (j e)").unsqueeze(2).to_broadcast([P, 2, ROTATED, DH]),
-                    op=ALU.mult,
-                )
-                by_pair = qk_ps[:].rearrange("p i (a j e) -> p i a j e", a=ROTATED, e=2)
-                crossed = rot_pool.tile([P, 2, 2, ROTATED, PAIRS], F32, name="crossed")
-                nc.vector.tensor_tensor(
-                    out=crossed[:, 0],
-                    in0=by_pair[:, :, :, :, 1],
-                    in1=d_neg[:, slots].unsqueeze(2).to_broadcast([P, 2, ROTATED, PAIRS]),
-                    op=ALU.mult,
-                )
-                nc.vector.tensor_tensor(
-                    out=crossed[:, 1],
-                    in0=by_pair[:, :, :, :, 0],
-                    in1=d_pos[:, slots].unsqueeze(2).to_broadcast([P, 2, ROTATED, PAIRS]),
-                    op=ALU.mult,
-                )
+        def rotation_products(group, half):
+            if half == 0:
+                live["result", group] = res_pool.tile([P, 3 * H, SLOTS, DH], F32, name="result")
+            first_slot = (group % GROUPS_PER_BATCH) * SLOTS + 2 * half
+            slots = slice(first_slot, first_slot + 2)
+            qk_ps = live["qk_ps", group, half]
+            rotated = live["result", group][:, 0:ROTATED, 2 * half : 2 * half + 2, :]
+            nc.vector.tensor_tensor(
+                out=rotated.rearrange("p a i d -> p i a d"),
+                in0=qk_ps[:].rearrange("p i (a d) -> p i a d", a=ROTATED),
+                in1=c_twice[:, slots]
+                .rearrange("p i j e -> p i (j e)")
+                .unsqueeze(2)
+                .to_broadcast([P, 2, ROTATED, DH]),
+                op=ALU.mult,
+            )
+            by_pair = qk_ps[:].rearrange("p i (a j e) -> p i a j e", a=ROTATED, e=2)
+            crossed = rot_pool.tile([P, 2, 2, ROTATED, PAIRS], F32, name="crossed")
+            nc.vector.tensor_tensor(
+                out=crossed[:, 0],
+                in0=by_pair[:, :, :, :, 1],
+                in1=d_neg[:, slots].unsqueeze(2).to_broadcast([P, 2, ROTATED, PAIRS]),
+                op=ALU.mult,
+            )
+            nc.vector.tensor_tensor(
+                out=crossed[:, 1],
+                in0=by_pair[:, :, :, :, 0],
+                in1=d_pos[:, slots].unsqueeze(2).to_broadcast([P, 2, ROTATED, PAIRS]),
+                op=ALU.mult,
+            )
+            live["crossed", group, half] = crossed
+
+        def copy_v(group):
+            nc.vector.tensor_copy(
+                out=live["result", group][:, ROTATED : 3 * H].rearrange("p a s d -> p s a d"),
+                in_=live["v_ps", group][:].rearrange("p s (a d) -> p s a d", a=H),
+            )
+
+        def rotation_sum(group):
+            for half in range(SLOTS // 2):
+                rotated = live["result", group][:, 0:ROTATED, 2 * half : 2 * half + 2, :]
                 nc.gpsimd.tensor_tensor(
                     out=rotated.rearrange("p a i (j e) -> p i a j e", e=2),
                     in0=rotated.rearrange("p a i (j e) -> p i a j e", e=2),
-                    in1=crossed[:].rearrange("p e i a j -> p i a j e"),
+                    in1=live["crossed", group, half][:].rearrange("p e i a j -> p i a j e"),
                     op=ALU.add,
                 )
 
-            nc.vector.tensor_copy(
-                out=result[:, ROTATED : 3 * H].rearrange("p a s d -> p s a d"),
-                in_=v_ps[:].rearrange("p s (a d) -> p s a d", a=H),
-            )
-
+        def store(group):
+            batch, first_slot = group // GROUPS_PER_BATCH, (group % GROUPS_PER_BATCH) * SLOTS
             for which in range(3):
                 by_slot = outs[which][batch].rearrange("h (p t) d -> p h t d", t=SLOTS_PER_BATCH)
                 nc.sync.dma_start(
                     out=by_slot[:, :, first_slot : first_slot + SLOTS, :],
-                    in_=result[:, which * H : (which + 1) * H],
+                    in_=live["result", group][:, which * H : (which + 1) * H],
                 )
+
+        def in_range(group):
+            return 0 <= group < GROUPS
+
+        with tc.manual_schedule():
+            for r in range(-1, GROUPS + 3):
+                if in_range(r + 1 + LOADS_AHEAD):
+                    load_group(r + 1 + LOADS_AHEAD)
+                if in_range(r):
+                    normalise(r)
+                if in_range(r + 1):
+                    statistics(r + 1)
+                if in_range(r - 1):
+                    transpose_and_scale(r - 1, 0)
+                if in_range(r + 1):
+                    standard_deviation(r + 1)
+                if in_range(r - 2):
+                    quantise(r - 2)
+                if in_range(r - 1):
+                    regroup(r - 1, 0)
+                    transpose_and_scale(r - 1, 1)
+                    regroup(r - 1, 1)
+                if in_range(r - 3):
+                    rotation_products(r - 3, 0)
+                if in_range(r + 1):
+                    token_scalars(r + 1)
+                if in_range(r - 3):
+                    rotation_products(r - 3, 1)
+                    copy_v(r - 3)
+                if in_range(r - 2):
+                    project(r - 2)
+                if in_range(r - 3):
+                    rotation_sum(r - 3)
+                    store(r - 3)

@@ -265,7 +265,7 @@ def tile_minitransformerlayer_pa_t_kernel(tc, x, pe, w_qkv, g1, b1, out_0, out_1
         def rotation_sum(group):
             for half in range(SLOTS // 2):
                 rotated = live["result", group][:, 0:ROTATED, 2 * half : 2 * half + 2, :]
-                nc.gpsimd.tensor_tensor(
+                nc.vector.tensor_tensor(
                     out=rotated.rearrange("p a i (j e) -> p i a j e", e=2),
                     in0=rotated.rearrange("p a i (j e) -> p i a j e", e=2),
                     in1=live["crossed", group, half][:].rearrange("p e i a j -> p i a j e"),

@@ -53,58 +53,71 @@ def tile_minitransformerlayer_pa_t_kernel(tc, x, pe, w_qkv, g1, b1, out_0, out_1
             batch, first_slot = group // GROUPS_PER_BATCH, (group % GROUPS_PER_BATCH) * SLOTS
             x_sb = x_pool.tile([P, SLOTS, D], BF16, name="x_sb")
             by_slot = x[batch].rearrange("(p t) k -> p t k", t=SLOTS_PER_BATCH)
-            nc.sync.dma_start(out=x_sb[:], in_=by_slot[:, first_slot : first_slot + SLOTS, :])
+            for s in range(SLOTS):
+                nc.sync.dma_start(out=x_sb[:, s, :], in_=by_slot[:, first_slot + s, :])
             live["x", group] = x_sb
 
-        for group in range(LOADS_AHEAD):
-            load_group(group)
+        xt_psum = ctx.enter_context(tc.psum_pool(name="xt_psum", bufs=4))
+        qk_psum = ctx.enter_context(tc.psum_pool(name="qk_psum", bufs=2))
+        v_psum = ctx.enter_context(tc.psum_pool(name="v_psum", bufs=2))
 
         ident_f32 = const.tile([P, P], F32, name="ident_f32")
-        make_identity(nc, ident_f32[:])
         ident_bf16 = const.tile([P, P], BF16, name="ident_bf16")
-        make_identity(nc, ident_bf16[:])
         eps = const.tile([P, 1], F32, name="eps")
-        nc.vector.memset(eps[:], EPS)
-
         gb_rows = const.tile([P, P], BF16, name="gb_rows")
-        nc.vector.memset(gb_rows[:], 0.0)
-        nc.sync.dma_start(out=gb_rows[0:CHUNKS, :], in_=g1.rearrange("(c p) -> c p", p=P))
-        nc.sync.dma_start(out=gb_rows[CHUNKS : 2 * CHUNKS, :], in_=b1.rearrange("(c p) -> c p", p=P))
         w_sb = const.tile([P, OUT_COLS // P, D], BF16, name="w_sb")
-        nc.sync.dma_start(out=w_sb[:], in_=w_qkv.rearrange("(i p) k -> p i k", p=P))
         pe_sb = const.tile([P, SLOTS_PER_BATCH, PAIRS, 2], BF16, name="pe_sb")
-        nc.sync.dma_start(out=pe_sb[:], in_=pe.rearrange("(p t) (j e) -> p t j e", t=SLOTS_PER_BATCH, e=2))
-
         c_twice = const.tile([P, SLOTS_PER_BATCH, PAIRS, 2], F32, name="c_twice")
-        nc.vector.tensor_copy(
-            out=c_twice[:], in_=pe_sb[:, :, :, 0:1].to_broadcast([P, SLOTS_PER_BATCH, PAIRS, 2])
-        )
         d_pos = const.tile([P, SLOTS_PER_BATCH, PAIRS], F32, name="d_pos")
-        nc.vector.tensor_copy(out=d_pos[:], in_=pe_sb[:, :, :, 1])
         d_neg = const.tile([P, SLOTS_PER_BATCH, PAIRS], F32, name="d_neg")
-        nc.vector.tensor_scalar_mul(out=d_neg[:], in0=pe_sb[:, :, :, 1], scalar1=-1.0)
-
         gain_bias = const.tile([P, 2 * CHUNKS], F32, name="gain_bias")
         w_grouped = const.tile([P, PASSES, OUT_COLS, PACK], BF16, name="w_grouped", align_bytes=64)
         w_codes = const.tile([P, PASSES, OUT_COLS], U32, name="w_codes", align_bytes=64)
         w_scales = const.tile([P, PASSES, OUT_COLS], U8, name="w_scales", align_bytes=64)
-        with tc.psum_pool(name="setup_psum", bufs=2) as setup_psum:
-            gb_cols = setup_psum.tile([P, P], BF16, name="gb_cols")
+
+        def load_constants():
+            nc.vector.memset(eps[:], EPS)
+            nc.vector.memset(gb_rows[:], 0.0)
+            nc.sync.dma_start(out=gb_rows[0:CHUNKS, :], in_=g1.rearrange("(c p) -> c p", p=P))
+            nc.sync.dma_start(out=gb_rows[CHUNKS : 2 * CHUNKS, :], in_=b1.rearrange("(c p) -> c p", p=P))
+            nc.sync.dma_start(out=w_sb[:], in_=w_qkv.rearrange("(i p) k -> p i k", p=P))
+            nc.sync.dma_start(
+                out=pe_sb[:], in_=pe.rearrange("(p t) (j e) -> p t j e", t=SLOTS_PER_BATCH, e=2)
+            )
+
+        def rotation_tables():
+            make_identity(nc, ident_bf16[:])
+            make_identity(nc, ident_f32[:])
+            nc.gpsimd.tensor_scalar(
+                out=c_twice[:],
+                in0=pe_sb[:, :, :, 0:1].to_broadcast([P, SLOTS_PER_BATCH, PAIRS, 2]),
+                scalar1=1.0,
+                scalar2=0.0,
+                op0=ALU.mult,
+                op1=ALU.add,
+            )
+            for table, sign in ((d_pos, 1.0), (d_neg, -1.0)):
+                nc.gpsimd.tensor_scalar(
+                    out=table[:], in0=pe_sb[:, :, :, 1], scalar1=sign, scalar2=0.0, op0=ALU.mult, op1=ALU.add
+                )
+
+        def transpose_constants():
+            gb_cols = xt_psum.tile([P, P], BF16, name="gb_cols", tag="xn_t")
             nc.tensor.transpose(gb_cols[:], gb_rows[:], ident_bf16[:])
             nc.vector.tensor_copy(out=gain_bias[:], in_=gb_cols[:, 0 : 2 * CHUNKS])
-
             for u in range(PASSES):
                 for i in range(OUT_COLS // P):
-                    rows = slice(i * P, (i + 1) * P)
-                    w_t = setup_psum.tile([P, PACK, P], BF16, name="w_t")
+                    w_t = xt_psum.tile([P, PACK, P], BF16, name="w_t", tag="xn_t")
                     for t in range(PACK):
                         chunk = u * PACK + t
                         nc.tensor.transpose(
                             w_t[:, t, :], w_sb[:, i, chunk * P : (chunk + 1) * P], ident_bf16[:]
                         )
-                    nc.vector.tensor_copy(
-                        out=w_grouped[:, u, rows, :], in_=w_t[:].rearrange("p t n -> p n t")
+                    nc.scalar.copy(
+                        out=w_grouped[:, u, i * P : (i + 1) * P, :], in_=w_t[:].rearrange("p t n -> p n t")
                     )
+
+        def quantise_weights():
             for u in range(PASSES):
                 for i in range(OUT_COLS // P):
                     rows = slice(i * P, (i + 1) * P)
@@ -113,10 +126,6 @@ def tile_minitransformerlayer_pa_t_kernel(tc, x, pe, w_qkv, g1, b1, out_0, out_1
                         scales=w_scales[:, u, rows],
                         in_=w_grouped[:, u, rows, :].rearrange("p n t -> p (n t)"),
                     )
-
-        xt_psum = ctx.enter_context(tc.psum_pool(name="xt_psum", bufs=4))
-        qk_psum = ctx.enter_context(tc.psum_pool(name="qk_psum", bufs=2))
-        v_psum = ctx.enter_context(tc.psum_pool(name="v_psum", bufs=2))
 
         def statistics(group):
             x_sb = live["x", group]
@@ -127,6 +136,7 @@ def tile_minitransformerlayer_pa_t_kernel(tc, x, pe, w_qkv, g1, b1, out_0, out_1
                     nc.vector.bn_stats(
                         out=stats[:, s, part, :], in_=x_sb[:, s, part * BN_MAX : (part + 1) * BN_MAX]
                     )
+            for s in range(SLOTS):
                 nc.vector.bn_aggr(out=mean_var[:, s, :], in_=stats[:, s].rearrange("p a c -> p (a c)"))
             live["mean_var", group] = mean_var
 
@@ -262,15 +272,14 @@ def tile_minitransformerlayer_pa_t_kernel(tc, x, pe, w_qkv, g1, b1, out_0, out_1
                 in_=live["v_ps", group][:].rearrange("p s (a d) -> p s a d", a=H),
             )
 
-        def rotation_sum(group):
-            for half in range(SLOTS // 2):
-                rotated = live["result", group][:, 0:ROTATED, 2 * half : 2 * half + 2, :]
-                nc.vector.tensor_tensor(
-                    out=rotated.rearrange("p a i (j e) -> p i a j e", e=2),
-                    in0=rotated.rearrange("p a i (j e) -> p i a j e", e=2),
-                    in1=live["crossed", group, half][:].rearrange("p e i a j -> p i a j e"),
-                    op=ALU.add,
-                )
+        def rotation_sum(group, half, engine):
+            rotated = live["result", group][:, 0:ROTATED, 2 * half : 2 * half + 2, :]
+            engine.tensor_tensor(
+                out=rotated.rearrange("p a i (j e) -> p i a j e", e=2),
+                in0=rotated.rearrange("p a i (j e) -> p i a j e", e=2),
+                in1=live["crossed", group, half][:].rearrange("p e i a j -> p i a j e"),
+                op=ALU.add,
+            )
 
         def store(group):
             batch, first_slot = group // GROUPS_PER_BATCH, (group % GROUPS_PER_BATCH) * SLOTS
@@ -285,7 +294,18 @@ def tile_minitransformerlayer_pa_t_kernel(tc, x, pe, w_qkv, g1, b1, out_0, out_1
             return 0 <= group < GROUPS
 
         with tc.manual_schedule():
-            for r in range(-1, GROUPS + 3):
+            load_group(0)
+            load_constants()
+            for group in range(1, 1 + LOADS_AHEAD):
+                load_group(group)
+            rotation_tables()
+            statistics(0)
+            standard_deviation(0)
+            token_scalars(0)
+            transpose_constants()
+            quantise_weights()
+
+            for r in range(GROUPS + 3):
                 if in_range(r + 1 + LOADS_AHEAD):
                     load_group(r + 1 + LOADS_AHEAD)
                 if in_range(r):
@@ -304,13 +324,14 @@ def tile_minitransformerlayer_pa_t_kernel(tc, x, pe, w_qkv, g1, b1, out_0, out_1
                     regroup(r - 1, 1)
                 if in_range(r - 3):
                     rotation_products(r - 3, 0)
+                    rotation_sum(r - 3, 0, nc.gpsimd)
                 if in_range(r + 1):
                     token_scalars(r + 1)
                 if in_range(r - 3):
                     rotation_products(r - 3, 1)
                     copy_v(r - 3)
+                    rotation_sum(r - 3, 1, nc.vector)
                 if in_range(r - 2):
                     project(r - 2)
                 if in_range(r - 3):
-                    rotation_sum(r - 3)
                     store(r - 3)

@@ -27,7 +27,6 @@ QK_COLS = ROTATED * DH
 V_COLS = H * DH
 OUT_COLS = QK_COLS + V_COLS
 BN_MAX = 512
-GROUPS = B * GROUPS_PER_BATCH
 LOADS_AHEAD = 2
 
 FLOPS = 2 * B * S * D * OUT_COLS
@@ -47,13 +46,22 @@ def tile_minitransformerlayer_pa_t_kernel(tc, x, pe, w_qkv, g1, b1, out_0, out_1
         rot_pool = ctx.enter_context(tc.tile_pool(name="rot_pool", bufs=4))
         res_pool = ctx.enter_context(tc.tile_pool(name="res_pool", bufs=3))
 
+        groups = []
+        for index in range(B * GROUPS_PER_BATCH):
+            batch, first_slot = index // GROUPS_PER_BATCH, (index % GROUPS_PER_BATCH) * SLOTS
+            if index in (0, B * GROUPS_PER_BATCH - 1):
+                groups.append((batch, first_slot, SLOTS // 2))
+                groups.append((batch, first_slot + SLOTS // 2, SLOTS // 2))
+            else:
+                groups.append((batch, first_slot, SLOTS))
+
         live = {}
 
         def load_group(group):
-            batch, first_slot = group // GROUPS_PER_BATCH, (group % GROUPS_PER_BATCH) * SLOTS
+            batch, first_slot, count = groups[group]
             x_sb = x_pool.tile([P, SLOTS, D], BF16, name="x_sb")
             by_slot = x[batch].rearrange("(p t) k -> p t k", t=SLOTS_PER_BATCH)
-            for s in range(SLOTS):
+            for s in range(count):
                 nc.sync.dma_start(out=x_sb[:, s, :], in_=by_slot[:, first_slot + s, :])
             live["x", group] = x_sb
 
@@ -128,36 +136,45 @@ def tile_minitransformerlayer_pa_t_kernel(tc, x, pe, w_qkv, g1, b1, out_0, out_1
                     )
 
         def statistics(group):
+            count = groups[group][2]
             x_sb = live["x", group]
             stats = small.tile([P, SLOTS, D // BN_MAX, 6], F32, name="stats")
             mean_var = small.tile([P, SLOTS, 2], F32, name="mean_var")
-            for s in range(SLOTS):
+            for s in range(count):
                 for part in range(D // BN_MAX):
                     nc.vector.bn_stats(
                         out=stats[:, s, part, :], in_=x_sb[:, s, part * BN_MAX : (part + 1) * BN_MAX]
                     )
-            for s in range(SLOTS):
+            for s in range(count):
                 nc.vector.bn_aggr(out=mean_var[:, s, :], in_=stats[:, s].rearrange("p a c -> p (a c)"))
             live["mean_var", group] = mean_var
 
         def standard_deviation(group):
+            count = groups[group][2]
             std = small.tile([P, SLOTS], F32, name="std")
             nc.scalar.activation(
-                out=std[:], in_=live["mean_var", group][:, :, 1], func=ACT.Sqrt, bias=eps[:], scale=1.0
+                out=std[:, 0:count],
+                in_=live["mean_var", group][:, 0:count, 1],
+                func=ACT.Sqrt,
+                bias=eps[:],
+                scale=1.0,
             )
             live["std", group] = std
 
         def token_scalars(group):
+            count = groups[group][2]
             rstd = small.tile([P, SLOTS], F32, name="rstd")
-            nc.vector.reciprocal(out=rstd[:], in_=live["std", group][:])
+            nc.vector.reciprocal(out=rstd[:, 0:count], in_=live["std", group][:, 0:count])
             neg_mean = small.tile([P, SLOTS], F32, name="neg_mean")
-            nc.vector.tensor_scalar_mul(out=neg_mean[:], in0=live["mean_var", group][:, :, 0], scalar1=-1.0)
+            nc.vector.tensor_scalar_mul(
+                out=neg_mean[:, 0:count], in0=live["mean_var", group][:, 0:count, 0], scalar1=-1.0
+            )
             live["rstd", group] = rstd
             live["neg_mean", group] = neg_mean
 
         def normalise(group):
             xn = xn_pool.tile([P, SLOTS, D], F32, name="xn")
-            for s in range(SLOTS):
+            for s in range(groups[group][2]):
                 nc.gpsimd.tensor_scalar(
                     out=xn[:, s, :],
                     in0=live["x", group][:, s, :],
@@ -168,43 +185,47 @@ def tile_minitransformerlayer_pa_t_kernel(tc, x, pe, w_qkv, g1, b1, out_0, out_1
                 )
             live["xn", group] = xn
 
-        def transpose_and_scale(group, u):
-            if u == 0:
+        def transpose_and_scale(group, chunks):
+            count = groups[group][2]
+            if chunks[0] == 0:
                 live["h_chunks", group] = h_pool.tile([P, CHUNKS, TOKENS], BF16, name="h_chunks")
-                live["h_grouped", group] = h_pool.tile(
-                    [P, PASSES, TOKENS, PACK], BF16, name="h_grouped", align_bytes=64
-                )
             xn, h_chunks = live["xn", group], live["h_chunks", group]
-            for c in range(u * PACK, (u + 1) * PACK):
+            for c in chunks:
                 xn_t = xt_psum.tile([P, TOKENS], F32, name="xn_t")
-                for s in range(SLOTS):
+                for s in range(count):
                     nc.tensor.transpose(
                         xn_t[:, s * P : (s + 1) * P], xn[:, s, c * P : (c + 1) * P], ident_f32[:]
                     )
                 nc.scalar.activation(
-                    out=h_chunks[:, c, :],
-                    in_=xn_t[:],
+                    out=h_chunks[:, c, 0 : count * P],
+                    in_=xn_t[:, 0 : count * P],
                     func=ACT.Identity,
                     scale=gain_bias[:, c : c + 1],
                     bias=gain_bias[:, CHUNKS + c : CHUNKS + c + 1],
                 )
 
         def regroup(group, u):
+            tokens = groups[group][2] * P
+            if u == 0:
+                live["h_grouped", group] = h_pool.tile(
+                    [P, PASSES, TOKENS, PACK], BF16, name="h_grouped", align_bytes=64
+                )
             nc.scalar.copy(
-                out=live["h_grouped", group][:, u].rearrange("p (n i) t -> p n t i", i=4),
-                in_=live["h_chunks", group][:, u * PACK : (u + 1) * PACK, :].rearrange(
+                out=live["h_grouped", group][:, u, 0:tokens, :].rearrange("p (n i) t -> p n t i", i=4),
+                in_=live["h_chunks", group][:, u * PACK : (u + 1) * PACK, 0:tokens].rearrange(
                     "p t (n i) -> p n t i", i=4
                 ),
             )
 
         def quantise(group):
+            tokens = groups[group][2] * P
             h_codes = mx_pool.tile([P, PASSES, TOKENS], U32, name="h_codes", align_bytes=64)
             h_scales = mx_pool.tile([P, PASSES, TOKENS], U8, name="h_scales", align_bytes=64)
             for u in range(PASSES):
                 nc.vector.quantize_mx(
-                    out=h_codes[:, u, :].bitcast(FP8X4),
-                    scales=h_scales[:, u, :],
-                    in_=live["h_grouped", group][:, u].rearrange("p n t -> p (n t)"),
+                    out=h_codes[:, u, 0:tokens].bitcast(FP8X4),
+                    scales=h_scales[:, u, 0:tokens],
+                    in_=live["h_grouped", group][:, u, 0:tokens, :].rearrange("p n t -> p (n t)"),
                 )
             live["h_codes", group] = h_codes
             live["h_scales", group] = h_scales
@@ -213,7 +234,7 @@ def tile_minitransformerlayer_pa_t_kernel(tc, x, pe, w_qkv, g1, b1, out_0, out_1
             h_codes, h_scales = live["h_codes", group], live["h_scales", group]
             v_ps = v_psum.tile([P, SLOTS, V_COLS], F32, name="v_ps")
             live["v_ps", group] = v_ps
-            for half in range(SLOTS // 2):
+            for half in range(groups[group][2] // 2):
                 qk_ps = qk_psum.tile([P, 2, QK_COLS], F32, name="qk_ps")
                 live["qk_ps", group, half] = qk_ps
                 for i in range(2):
@@ -237,7 +258,7 @@ def tile_minitransformerlayer_pa_t_kernel(tc, x, pe, w_qkv, g1, b1, out_0, out_1
         def rotation_products(group, half):
             if half == 0:
                 live["result", group] = res_pool.tile([P, 3 * H, SLOTS, DH], F32, name="result")
-            first_slot = (group % GROUPS_PER_BATCH) * SLOTS + 2 * half
+            first_slot = groups[group][1] + 2 * half
             slots = slice(first_slot, first_slot + 2)
             qk_ps = live["qk_ps", group, half]
             rotated = live["result", group][:, 0:ROTATED, 2 * half : 2 * half + 2, :]
@@ -266,12 +287,6 @@ def tile_minitransformerlayer_pa_t_kernel(tc, x, pe, w_qkv, g1, b1, out_0, out_1
             )
             live["crossed", group, half] = crossed
 
-        def copy_v(group):
-            nc.vector.tensor_copy(
-                out=live["result", group][:, ROTATED : 3 * H].rearrange("p a s d -> p s a d"),
-                in_=live["v_ps", group][:].rearrange("p s (a d) -> p s a d", a=H),
-            )
-
         def rotation_sum(group, half, engine):
             rotated = live["result", group][:, 0:ROTATED, 2 * half : 2 * half + 2, :]
             engine.tensor_tensor(
@@ -281,17 +296,27 @@ def tile_minitransformerlayer_pa_t_kernel(tc, x, pe, w_qkv, g1, b1, out_0, out_1
                 op=ALU.add,
             )
 
+        def copy_v(group):
+            count = groups[group][2]
+            nc.vector.tensor_copy(
+                out=live["result", group][:, ROTATED : 3 * H, 0:count, :].rearrange("p a s d -> p s a d"),
+                in_=live["v_ps", group][:, 0:count, :].rearrange("p s (a d) -> p s a d", a=H),
+            )
+
         def store(group):
-            batch, first_slot = group // GROUPS_PER_BATCH, (group % GROUPS_PER_BATCH) * SLOTS
+            batch, first_slot, count = groups[group]
             for which in range(3):
                 by_slot = outs[which][batch].rearrange("h (p t) d -> p h t d", t=SLOTS_PER_BATCH)
                 nc.sync.dma_start(
-                    out=by_slot[:, :, first_slot : first_slot + SLOTS, :],
-                    in_=live["result", group][:, which * H : (which + 1) * H],
+                    out=by_slot[:, :, first_slot : first_slot + count, :],
+                    in_=live["result", group][:, which * H : (which + 1) * H, 0:count, :],
                 )
 
         def in_range(group):
-            return 0 <= group < GROUPS
+            return 0 <= group < len(groups)
+
+        def is_whole(group):
+            return in_range(group) and groups[group][2] == SLOTS
 
         with tc.manual_schedule():
             load_group(0)
@@ -305,7 +330,7 @@ def tile_minitransformerlayer_pa_t_kernel(tc, x, pe, w_qkv, g1, b1, out_0, out_1
             transpose_constants()
             quantise_weights()
 
-            for r in range(GROUPS + 3):
+            for r in range(len(groups) + 3):
                 if in_range(r + 1 + LOADS_AHEAD):
                     load_group(r + 1 + LOADS_AHEAD)
                 if in_range(r):
@@ -313,23 +338,25 @@ def tile_minitransformerlayer_pa_t_kernel(tc, x, pe, w_qkv, g1, b1, out_0, out_1
                 if in_range(r + 1):
                     statistics(r + 1)
                 if in_range(r - 1):
-                    transpose_and_scale(r - 1, 0)
+                    transpose_and_scale(r - 1, range(0, PACK + 1))
                 if in_range(r + 1):
                     standard_deviation(r + 1)
                 if in_range(r - 2):
                     quantise(r - 2)
                 if in_range(r - 1):
                     regroup(r - 1, 0)
-                    transpose_and_scale(r - 1, 1)
+                    transpose_and_scale(r - 1, range(PACK + 1, CHUNKS))
                     regroup(r - 1, 1)
                 if in_range(r - 3):
                     rotation_products(r - 3, 0)
                     rotation_sum(r - 3, 0, nc.gpsimd)
                 if in_range(r + 1):
                     token_scalars(r + 1)
-                if in_range(r - 3):
+                if is_whole(r - 3):
                     rotation_products(r - 3, 1)
+                if in_range(r - 3):
                     copy_v(r - 3)
+                if is_whole(r - 3):
                     rotation_sum(r - 3, 1, nc.vector)
                 if in_range(r - 2):
                     project(r - 2)

@@ -27,6 +27,7 @@ QK_COLS = ROTATED * DH
 V_COLS = H * DH
 OUT_COLS = QK_COLS + V_COLS
 BN_MAX = 512
+BN_VALUES = 6
 LOADS_AHEAD = 2
 
 FLOPS = 2 * B * S * D * OUT_COLS
@@ -138,7 +139,7 @@ def tile_minitransformerlayer_pa_t_kernel(tc, x, pe, w_qkv, g1, b1, out_0, out_1
         def statistics(group):
             count = groups[group][2]
             x_sb = live["x", group]
-            stats = small.tile([P, SLOTS, D // BN_MAX, 6], F32, name="stats")
+            stats = small.tile([P, SLOTS, D // BN_MAX, BN_VALUES], F32, name="stats")
             mean_var = small.tile([P, SLOTS, 2], F32, name="mean_var")
             for s in range(count):
                 for part in range(D // BN_MAX):
@@ -161,15 +162,23 @@ def tile_minitransformerlayer_pa_t_kernel(tc, x, pe, w_qkv, g1, b1, out_0, out_1
             )
             live["std", group] = std
 
-        def token_scalars(group):
+        def reciprocal_std(group):
             count = groups[group][2]
             rstd = small.tile([P, SLOTS], F32, name="rstd")
             nc.vector.reciprocal(out=rstd[:, 0:count], in_=live["std", group][:, 0:count])
-            neg_mean = small.tile([P, SLOTS], F32, name="neg_mean")
-            nc.vector.tensor_scalar_mul(
-                out=neg_mean[:, 0:count], in0=live["mean_var", group][:, 0:count, 0], scalar1=-1.0
-            )
             live["rstd", group] = rstd
+
+        def negated_mean(group):
+            count = groups[group][2]
+            neg_mean = small.tile([P, SLOTS], F32, name="neg_mean")
+            nc.gpsimd.tensor_scalar(
+                out=neg_mean[:, 0:count],
+                in0=live["mean_var", group][:, 0:count, 0],
+                scalar1=-1.0,
+                scalar2=0.0,
+                op0=ALU.mult,
+                op1=ALU.add,
+            )
             live["neg_mean", group] = neg_mean
 
         def normalise(group):
@@ -325,8 +334,9 @@ def tile_minitransformerlayer_pa_t_kernel(tc, x, pe, w_qkv, g1, b1, out_0, out_1
                 load_group(group)
             rotation_tables()
             statistics(0)
+            negated_mean(0)
             standard_deviation(0)
-            token_scalars(0)
+            reciprocal_std(0)
             transpose_constants()
             quantise_weights()
 
@@ -337,28 +347,29 @@ def tile_minitransformerlayer_pa_t_kernel(tc, x, pe, w_qkv, g1, b1, out_0, out_1
                     normalise(r)
                 if in_range(r + 1):
                     statistics(r + 1)
+                    negated_mean(r + 1)
                 if in_range(r - 1):
-                    transpose_and_scale(r - 1, range(0, PACK + 1))
+                    transpose_and_scale(r - 1, range(CHUNKS))
                 if in_range(r + 1):
                     standard_deviation(r + 1)
                 if in_range(r - 2):
                     quantise(r - 2)
+                if is_whole(r - 4):
+                    rotation_sum(r - 4, 1, nc.vector)
+                    store(r - 4)
                 if in_range(r - 1):
                     regroup(r - 1, 0)
-                    transpose_and_scale(r - 1, range(PACK + 1, CHUNKS))
                     regroup(r - 1, 1)
                 if in_range(r - 3):
                     rotation_products(r - 3, 0)
                     rotation_sum(r - 3, 0, nc.gpsimd)
                 if in_range(r + 1):
-                    token_scalars(r + 1)
+                    reciprocal_std(r + 1)
                 if is_whole(r - 3):
                     rotation_products(r - 3, 1)
                 if in_range(r - 3):
                     copy_v(r - 3)
-                if is_whole(r - 3):
-                    rotation_sum(r - 3, 1, nc.vector)
                 if in_range(r - 2):
                     project(r - 2)
-                if in_range(r - 3):
+                if in_range(r - 3) and not is_whole(r - 3):
                     store(r - 3)

from contextlib import ExitStack

import concourse.mybir as mybir
from concourse.masks import make_identity

F32 = mybir.dt.float32
BF16 = mybir.dt.bfloat16
U32 = mybir.dt.uint32
U8 = mybir.dt.uint8
FP8X4 = mybir.dt.float8_e4m3fn_x4
ALU = mybir.AluOpType
ACT = mybir.ActivationFunctionType

B, S, D, H, DH = 4, 2048, 1024, 2, 64
EPS = 1e-5
P = 128
PACK = 4
PASSES = D // (P * PACK)
CHUNKS = D // P
SLOTS_PER_BATCH = S // P
SLOTS = 4
TOKENS = SLOTS * P
GROUPS_PER_BATCH = SLOTS_PER_BATCH // SLOTS
PAIRS = DH // 2
ROTATED = 2 * H
QK_COLS = ROTATED * DH
V_COLS = H * DH
OUT_COLS = QK_COLS + V_COLS
BN_MAX = 512
BN_VALUES = 6
LOADS_AHEAD = 2

FLOPS = 2 * B * S * D * OUT_COLS


def tile_minitransformerlayer_pa_t_kernel(tc, x, pe, w_qkv, g1, b1, out_0, out_1, out_2):
    nc = tc.nc
    outs = (out_0, out_1, out_2)

    with ExitStack() as ctx:
        const = ctx.enter_context(tc.tile_pool(name="const", bufs=1))
        x_pool = ctx.enter_context(tc.tile_pool(name="x_pool", bufs=4))
        small = ctx.enter_context(tc.tile_pool(name="small", bufs=3))
        xn_pool = ctx.enter_context(tc.tile_pool(name="xn_pool", bufs=2))
        h_pool = ctx.enter_context(tc.tile_pool(name="h_pool", bufs=2))
        mx_pool = ctx.enter_context(tc.tile_pool(name="mx_pool", bufs=2))
        rot_pool = ctx.enter_context(tc.tile_pool(name="rot_pool", bufs=4))
        res_pool = ctx.enter_context(tc.tile_pool(name="res_pool", bufs=3))

        groups = []
        for index in range(B * GROUPS_PER_BATCH):
            batch, first_slot = index // GROUPS_PER_BATCH, (index % GROUPS_PER_BATCH) * SLOTS
            if index in (0, B * GROUPS_PER_BATCH - 1):
                groups.append((batch, first_slot, SLOTS // 2))
                groups.append((batch, first_slot + SLOTS // 2, SLOTS // 2))
            else:
                groups.append((batch, first_slot, SLOTS))

        live = {}

        def load_group(group):
            batch, first_slot, count = groups[group]
            x_sb = x_pool.tile([P, SLOTS, D], BF16, name="x_sb")
            by_slot = x[batch].rearrange("(p t) k -> p t k", t=SLOTS_PER_BATCH)
            for s in range(count):
                nc.sync.dma_start(out=x_sb[:, s, :], in_=by_slot[:, first_slot + s, :])
            live["x", group] = x_sb

        xt_psum = ctx.enter_context(tc.psum_pool(name="xt_psum", bufs=4))
        qk_psum = ctx.enter_context(tc.psum_pool(name="qk_psum", bufs=2))
        v_psum = ctx.enter_context(tc.psum_pool(name="v_psum", bufs=2))

        ident_f32 = const.tile([P, P], F32, name="ident_f32")
        ident_bf16 = const.tile([P, P], BF16, name="ident_bf16")
        eps = const.tile([P, 1], F32, name="eps")
        gb_rows = const.tile([P, P], BF16, name="gb_rows")
        w_sb = const.tile([P, OUT_COLS // P, D], BF16, name="w_sb")
        pe_sb = const.tile([P, SLOTS_PER_BATCH, PAIRS, 2], BF16, name="pe_sb")
        c_twice = const.tile([P, SLOTS_PER_BATCH, PAIRS, 2], F32, name="c_twice")
        d_pos = const.tile([P, SLOTS_PER_BATCH, PAIRS], F32, name="d_pos")
        d_neg = const.tile([P, SLOTS_PER_BATCH, PAIRS], F32, name="d_neg")
        gain_bias = const.tile([P, 2 * CHUNKS], F32, name="gain_bias")
        w_grouped = const.tile([P, PASSES, OUT_COLS, PACK], BF16, name="w_grouped", align_bytes=64)
        w_codes = const.tile([P, PASSES, OUT_COLS], U32, name="w_codes", align_bytes=64)
        w_scales = const.tile([P, PASSES, OUT_COLS], U8, name="w_scales", align_bytes=64)

        def load_constants():
            nc.vector.memset(eps[:], EPS)
            nc.vector.memset(gb_rows[:], 0.0)
            nc.sync.dma_start(out=gb_rows[0:CHUNKS, :], in_=g1.rearrange("(c p) -> c p", p=P))
            nc.sync.dma_start(out=gb_rows[CHUNKS : 2 * CHUNKS, :], in_=b1.rearrange("(c p) -> c p", p=P))
            nc.sync.dma_start(out=w_sb[:], in_=w_qkv.rearrange("(i p) k -> p i k", p=P))
            nc.sync.dma_start(
                out=pe_sb[:], in_=pe.rearrange("(p t) (j e) -> p t j e", t=SLOTS_PER_BATCH, e=2)
            )

        def rotation_tables():
            make_identity(nc, ident_bf16[:])
            make_identity(nc, ident_f32[:])
            nc.gpsimd.tensor_scalar(
                out=c_twice[:],
                in0=pe_sb[:, :, :, 0:1].to_broadcast([P, SLOTS_PER_BATCH, PAIRS, 2]),
                scalar1=1.0,
                scalar2=0.0,
                op0=ALU.mult,
                op1=ALU.add,
            )
            for table, sign in ((d_pos, 1.0), (d_neg, -1.0)):
                nc.gpsimd.tensor_scalar(
                    out=table[:], in0=pe_sb[:, :, :, 1], scalar1=sign, scalar2=0.0, op0=ALU.mult, op1=ALU.add
                )

        def transpose_constants():
            gb_cols = xt_psum.tile([P, P], BF16, name="gb_cols", tag="xn_t")
            nc.tensor.transpose(gb_cols[:], gb_rows[:], ident_bf16[:])
            nc.vector.tensor_copy(out=gain_bias[:], in_=gb_cols[:, 0 : 2 * CHUNKS])
            for u in range(PASSES):
                for i in range(OUT_COLS // P):
                    w_t = xt_psum.tile([P, PACK, P], BF16, name="w_t", tag="xn_t")
                    for t in range(PACK):
                        chunk = u * PACK + t
                        nc.tensor.transpose(
                            w_t[:, t, :], w_sb[:, i, chunk * P : (chunk + 1) * P], ident_bf16[:]
                        )
                    nc.scalar.copy(
                        out=w_grouped[:, u, i * P : (i + 1) * P, :], in_=w_t[:].rearrange("p t n -> p n t")
                    )

        def quantise_weights():
            for u in range(PASSES):
                for i in range(OUT_COLS // P):
                    rows = slice(i * P, (i + 1) * P)
                    nc.vector.quantize_mx(
                        out=w_codes[:, u, rows].bitcast(FP8X4),
                        scales=w_scales[:, u, rows],
                        in_=w_grouped[:, u, rows, :].rearrange("p n t -> p (n t)"),
                    )

        def statistics(group):
            count = groups[group][2]
            x_sb = live["x", group]
            stats = small.tile([P, SLOTS, D // BN_MAX, BN_VALUES], F32, name="stats")
            mean_var = small.tile([P, SLOTS, 2], F32, name="mean_var")
            for s in range(count):
                for part in range(D // BN_MAX):
                    nc.vector.bn_stats(
                        out=stats[:, s, part, :], in_=x_sb[:, s, part * BN_MAX : (part + 1) * BN_MAX]
                    )
            for s in range(count):
                nc.vector.bn_aggr(out=mean_var[:, s, :], in_=stats[:, s].rearrange("p a c -> p (a c)"))
            live["mean_var", group] = mean_var

        def standard_deviation(group):
            count = groups[group][2]
            std = small.tile([P, SLOTS], F32, name="std")
            nc.scalar.activation(
                out=std[:, 0:count],
                in_=live["mean_var", group][:, 0:count, 1],
                func=ACT.Sqrt,
                bias=eps[:],
                scale=1.0,
            )
            live["std", group] = std

        def reciprocal_std(group):
            count = groups[group][2]
            rstd = small.tile([P, SLOTS], F32, name="rstd")
            nc.vector.reciprocal(out=rstd[:, 0:count], in_=live["std", group][:, 0:count])
            live["rstd", group] = rstd

        def negated_mean(group):
            count = groups[group][2]
            neg_mean = small.tile([P, SLOTS], F32, name="neg_mean")
            nc.gpsimd.tensor_scalar(
                out=neg_mean[:, 0:count],
                in0=live["mean_var", group][:, 0:count, 0],
                scalar1=-1.0,
                scalar2=0.0,
                op0=ALU.mult,
                op1=ALU.add,
            )
            live["neg_mean", group] = neg_mean

        def normalise(group):
            xn = xn_pool.tile([P, SLOTS, D], F32, name="xn")
            for s in range(groups[group][2]):
                nc.gpsimd.tensor_scalar(
                    out=xn[:, s, :],
                    in0=live["x", group][:, s, :],
                    scalar1=live["neg_mean", group][:, s : s + 1],
                    scalar2=live["rstd", group][:, s : s + 1],
                    op0=ALU.add,
                    op1=ALU.mult,
                )
            live["xn", group] = xn

        def transpose_and_scale(group, chunks):
            count = groups[group][2]
            if chunks[0] == 0:
                live["h_chunks", group] = h_pool.tile([P, CHUNKS, TOKENS], BF16, name="h_chunks")
            xn, h_chunks = live["xn", group], live["h_chunks", group]
            for c in chunks:
                xn_t = xt_psum.tile([P, TOKENS], F32, name="xn_t")
                for s in range(count):
                    nc.tensor.transpose(
                        xn_t[:, s * P : (s + 1) * P], xn[:, s, c * P : (c + 1) * P], ident_f32[:]
                    )
                nc.scalar.activation(
                    out=h_chunks[:, c, 0 : count * P],
                    in_=xn_t[:, 0 : count * P],
                    func=ACT.Identity,
                    scale=gain_bias[:, c : c + 1],
                    bias=gain_bias[:, CHUNKS + c : CHUNKS + c + 1],
                )

        def regroup(group, u):
            tokens = groups[group][2] * P
            if u == 0:
                live["h_grouped", group] = h_pool.tile(
                    [P, PASSES, TOKENS, PACK], BF16, name="h_grouped", align_bytes=64
                )
            nc.scalar.copy(
                out=live["h_grouped", group][:, u, 0:tokens, :].rearrange("p (n i) t -> p n t i", i=4),
                in_=live["h_chunks", group][:, u * PACK : (u + 1) * PACK, 0:tokens].rearrange(
                    "p t (n i) -> p n t i", i=4
                ),
            )

        def quantise(group):
            tokens = groups[group][2] * P
            h_codes = mx_pool.tile([P, PASSES, TOKENS], U32, name="h_codes", align_bytes=64)
            h_scales = mx_pool.tile([P, PASSES, TOKENS], U8, name="h_scales", align_bytes=64)
            for u in range(PASSES):
                nc.vector.quantize_mx(
                    out=h_codes[:, u, 0:tokens].bitcast(FP8X4),
                    scales=h_scales[:, u, 0:tokens],
                    in_=live["h_grouped", group][:, u, 0:tokens, :].rearrange("p n t -> p (n t)"),
                )
            live["h_codes", group] = h_codes
            live["h_scales", group] = h_scales

        def project(group):
            h_codes, h_scales = live["h_codes", group], live["h_scales", group]
            v_ps = v_psum.tile([P, SLOTS, V_COLS], F32, name="v_ps")
            live["v_ps", group] = v_ps
            for half in range(groups[group][2] // 2):
                qk_ps = qk_psum.tile([P, 2, QK_COLS], F32, name="qk_ps")
                live["qk_ps", group, half] = qk_ps
                for i in range(2):
                    s = 2 * half + i
                    tokens = slice(s * P, (s + 1) * P)
                    for acc, cols in (
                        (qk_ps[:, i, :], slice(0, QK_COLS)),
                        (v_ps[:, s, :], slice(QK_COLS, OUT_COLS)),
                    ):
                        for u in range(PASSES):
                            nc.tensor.matmul_mx(
                                out=acc,
                                lhsT=h_codes[:, u, tokens].bitcast(FP8X4),
                                lhsT_scale=h_scales[:, u, tokens],
                                rhs=w_codes[:, u, cols].bitcast(FP8X4),
                                rhs_scale=w_scales[:, u, cols],
                                start=(u == 0),
                                stop=(u == PASSES - 1),
                            )

        def rotation_products(group, half):
            if half == 0:
                live["result", group] = res_pool.tile([P, 3 * H, SLOTS, DH], F32, name="result")
            first_slot = groups[group][1] + 2 * half
            slots = slice(first_slot, first_slot + 2)
            qk_ps = live["qk_ps", group, half]
            rotated = live["result", group][:, 0:ROTATED, 2 * half : 2 * half + 2, :]
            nc.vector.tensor_tensor(
                out=rotated.rearrange("p a i d -> p i a d"),
                in0=qk_ps[:].rearrange("p i (a d) -> p i a d", a=ROTATED),
                in1=c_twice[:, slots]
                .rearrange("p i j e -> p i (j e)")
                .unsqueeze(2)
                .to_broadcast([P, 2, ROTATED, DH]),
                op=ALU.mult,
            )
            by_pair = qk_ps[:].rearrange("p i (a j e) -> p i a j e", a=ROTATED, e=2)
            crossed = rot_pool.tile([P, 2, 2, ROTATED, PAIRS], F32, name="crossed")
            nc.vector.tensor_tensor(
                out=crossed[:, 0],
                in0=by_pair[:, :, :, :, 1],
                in1=d_neg[:, slots].unsqueeze(2).to_broadcast([P, 2, ROTATED, PAIRS]),
                op=ALU.mult,
            )
            nc.vector.tensor_tensor(
                out=crossed[:, 1],
                in0=by_pair[:, :, :, :, 0],
                in1=d_pos[:, slots].unsqueeze(2).to_broadcast([P, 2, ROTATED, PAIRS]),
                op=ALU.mult,
            )
            live["crossed", group, half] = crossed

        def rotation_sum(group, half, engine):
            rotated = live["result", group][:, 0:ROTATED, 2 * half : 2 * half + 2, :]
            engine.tensor_tensor(
                out=rotated.rearrange("p a i (j e) -> p i a j e", e=2),
                in0=rotated.rearrange("p a i (j e) -> p i a j e", e=2),
                in1=live["crossed", group, half][:].rearrange("p e i a j -> p i a j e"),
                op=ALU.add,
            )

        def copy_v(group):
            count = groups[group][2]
            nc.vector.tensor_copy(
                out=live["result", group][:, ROTATED : 3 * H, 0:count, :].rearrange("p a s d -> p s a d"),
                in_=live["v_ps", group][:, 0:count, :].rearrange("p s (a d) -> p s a d", a=H),
            )

        def store(group):
            batch, first_slot, count = groups[group]
            for which in range(3):
                by_slot = outs[which][batch].rearrange("h (p t) d -> p h t d", t=SLOTS_PER_BATCH)
                nc.sync.dma_start(
                    out=by_slot[:, :, first_slot : first_slot + count, :],
                    in_=live["result", group][:, which * H : (which + 1) * H, 0:count, :],
                )

        def in_range(group):
            return 0 <= group < len(groups)

        def is_whole(group):
            return in_range(group) and groups[group][2] == SLOTS

        with tc.manual_schedule():
            load_group(0)
            load_constants()
            for group in range(1, 1 + LOADS_AHEAD):
                load_group(group)
            rotation_tables()
            statistics(0)
            negated_mean(0)
            standard_deviation(0)
            reciprocal_std(0)
            transpose_constants()
            quantise_weights()

            for r in range(len(groups) + 3):
                if in_range(r + 1 + LOADS_AHEAD):
                    load_group(r + 1 + LOADS_AHEAD)
                if in_range(r):
                    normalise(r)
                if in_range(r + 1):
                    statistics(r + 1)
                    negated_mean(r + 1)
                if in_range(r - 1):
                    transpose_and_scale(r - 1, range(CHUNKS))
                if in_range(r + 1):
                    standard_deviation(r + 1)
                if in_range(r - 2):
                    quantise(r - 2)
                if is_whole(r - 4):
                    rotation_sum(r - 4, 1, nc.vector)
                    store(r - 4)
                if in_range(r - 1):
                    regroup(r - 1, 0)
                    regroup(r - 1, 1)
                if in_range(r - 3):
                    rotation_products(r - 3, 0)
                    rotation_sum(r - 3, 0, nc.gpsimd)
                if in_range(r + 1):
                    reciprocal_std(r + 1)
                if is_whole(r - 3):
                    rotation_products(r - 3, 1)
                if in_range(r - 3):
                    copy_v(r - 3)
                if in_range(r - 2):
                    project(r - 2)
                if in_range(r - 3) and not is_whole(r - 3):
                    store(r - 3)
